import numpy as np
import ml_dtypes


def mxq(x, axis, fmt="e4m3"):
    dtype, down = {"e4m3": (ml_dtypes.float8_e4m3fn, 7), "e5m2": (ml_dtypes.float8_e5m2, 14)}[fmt]
    v = np.moveaxis(np.asarray(x, np.float32).astype(ml_dtypes.bfloat16).astype(np.float64), axis, -1)
    blocks = v.reshape(v.shape[:-1] + (-1, 32))
    amax = np.abs(blocks).max(-1, keepdims=True)
    byte = np.maximum(np.where(amax > 0, np.frexp(amax)[1] - 1 + 127, 0) - down, 1)
    scale = np.exp2(byte - 127.0)
    codes = (blocks / scale).astype(np.float32).astype(dtype).astype(np.float64)
    return np.moveaxis((codes * scale).reshape(v.shape), -1, axis)


WIDE = False


def mx_kscale(k):
    if not WIDE:
        return np.ones(k)
    levels = np.array([10, -10, 5, -5, 0])
    if k % 512:
        return np.exp2(np.random.permutation(np.resize(levels, k // 32))).repeat(32)
    a = np.empty((k // 512, 16))
    for p in range(k // 512):
        a[p, :8] = np.random.permutation(np.resize(levels, 8))
        for g in range(8):
            far = levels[np.abs(levels - a[p, g]) >= 10]
            a[p, g + 8] = far[np.random.randint(len(far))]
    return np.exp2(a.ravel()).repeat(32)


BF16 = ml_dtypes.bfloat16


def bf(x):
    return np.asarray(x, np.float32).astype(BF16)


def f64(x):
    return np.asarray(x).astype(np.float64)


IN_C, OUT_C, N, ND = 512, 1024, 512, 2


def sigmoid(v):
    return 1.0 / (1.0 + np.exp(-v))


def setup_inputs():
    s, t = mx_kscale(IN_C), mx_kscale(OUT_C)
    rn = np.random.standard_normal
    return {"x": bf(rn((IN_C, N)) * s[:, None]),
            "h_prev_dim0": bf(rn((OUT_C, N)) * t[:, None]),
            "h_prev_dim1": bf(rn((OUT_C, N)) * t[:, None]),
            "ct0": bf(rn((OUT_C, N)) * 0.65),
            "ct1": bf(rn((OUT_C, N)) * 0.65),
            "w_io": bf(rn((OUT_C, IN_C)) * 0.7 / np.sqrt(IN_C) / s[None, :]),
            "w_ho": bf(rn((OUT_C, OUT_C)) * 0.7 / np.sqrt(OUT_C) / t[None, :]),
            "b_o": bf(rn((OUT_C, 1)) * 0.5),
            "weighted_sum": bf(0.4 + 0.5 * np.random.random(ND))}


def core(x, h_prev_dim0, h_prev_dim1, ct0, ct1, w_io, w_ho, b_o, weighted_sum):
    xo = mxq(f64(w_io), 1, "e4m3") @ mxq(f64(x), 0, "e4m3")
    who = mxq(f64(w_ho), 1, "e4m3")
    ws = f64(weighted_sum)

    def hidden(h_prev, c):
        o = sigmoid(xo + (who @ mxq(f64(h_prev), 0, "e4m3")) + f64(b_o))
        return o * np.tanh(f64(c))

    ht0 = hidden(h_prev_dim0, ct0)
    ht1 = hidden(h_prev_dim1, ct1)
    return ht0 * ws[0] + ht1 * ws[1]


def e4m3fn_bytes(y):
    return np.clip(np.asarray(y, np.float64), -448.0, 448.0).astype(np.float32).astype(ml_dtypes.float8_e4m3fn).view(np.uint8)


def reference(x, h_prev_dim0, h_prev_dim1, ct0, ct1, w_io, w_ho, b_o, weighted_sum):
    out = core(x, h_prev_dim0, h_prev_dim1, ct0, ct1, w_io, w_ho, b_o, weighted_sum)
    s = np.max(np.abs(out)) / 448.0
    return out, e4m3fn_bytes(out / s)

@@ -1,0 +1,240 @@
+from contextlib import ExitStack
+
+import concourse.mybir as mybir
+from concourse.masks import make_identity
+
+IN_C, OUT_C, N = 512, 1024, 512
+FLOPS = 2 * OUT_C * IN_C * N + 2 * 2 * OUT_C * OUT_C * N
+
+F32 = mybir.dt.float32
+BF16 = mybir.dt.bfloat16
+U32 = mybir.dt.uint32
+U8 = mybir.dt.uint8
+FP8X4 = mybir.dt.float8_e4m3fn_x4
+FP8 = mybir.dt.float8_e4m3fn
+ACT = mybir.ActivationFunctionType
+ALU = mybir.AluOpType
+AX = mybir.AxisListType
+
+P = 128
+A = OUT_C // P
+NV = 400
+WC_ON_VECTOR = ()
+CASTS = (("v", 0, 1024), ("s", 2752, 3424), ("v", 1024, 2048), ("s", 3424, 4096), ("v", 2048, 2752))
+LOADS = ("u0", "wh0", "u1", "wi0", "u2", "c0_0", "sm0", "u3", "u4", "c1_0", "wh1", "wi1", "c0_1", "c1_1", "wh2", "wi2", "c0_2", "c1_2", "wh3", "wi3", "c0_3", "c1_3")
+ORDER = ("ILV_0", "ILS_0", "TH_0", "QU_0", "TH_1", "WCH_0", "ILV_1", "ILS_1", "TI_0", "WCH_1", "QU_1", "WCI_0", "ILV_2", "ILS_2", "TANH_0_0", "QWI_0", "QWH_0", "ILS_3", "QU_2", "ILS_4", "ILV_3", "MM_0_0", "TANH_0_1", "MM_1_0", "ILV_4", "SG_0_0", "TH_2", "SG_1_0", "QU_3", "TH_3", "WCH_2", "QU_4", "WCH_3", "TI_1", "ST_0_0", "TANH_1_0", "TH_4", "QWH_1", "MM_0_1", "ST_1_0", "WCI_1", "WCH_4", "MM_1_1", "QWI_1", "SG_0_1", "TH_5", "SG_1_1", "ST_0_1", "TI_2", "WCH_5", "ST_1_1", "MM_2_0", "WCI_2", "AD_0", "TANH_1_1", "TH_6", "AD_1", "TH_7", "RD_0", "SG_2_0", "RD_1", "MM_3_0", "WCH_6", "QWI_2", "MM_2_1", "QWH_2", "SG_3_0", "ST_2_0", "WCH_7", "TI_3", "ST_3_0", "SG_2_1", "MM_3_1", "QWH_3", "WCI_3", "MM_4_0", "ST_2_1", "SG_3_1", "QWI_3", "TANH_2_0", "MM_5_0", "AD_2", "ST_3_1", "MM_4_1", "SG_4_0", "RD_2", "SG_5_0", "MM_5_1", "AD_3", "TANH_2_1", "ST_4_0", "MM_6_0", "RD_3", "SG_4_1", "MM_7_0", "ST_5_0", "SG_5_1", "ST_4_1", "MM_6_1", "TANH_3_0", "ST_5_1", "MM_7_1", "AD_4", "SG_6_0", "AD_5", "SG_7_0", "RD_4", "TANH_3_1", "RD_5", "ST_6_0", "SG_6_1", "ST_7_0", "SG_7_1", "ST_6_1", "ST_7_1", "AD_6", "AD_7", "RD_6", "RD_7")
+MANUAL = True
+
+
+def tile_mdlstmcellweights_pb_kernel(
+    tc, x, h_prev_dim0, h_prev_dim1, ct0, ct1, w_io, w_ho, b_o, weighted_sum, out_0, out_1
+):
+    nc = tc.nc
+    with ExitStack() as ctx:
+        keep = ctx.enter_context(tc.tile_pool(name="keep", bufs=1))
+        op = ctx.enter_context(tc.tile_pool(name="op", bufs=6))
+        pp = ctx.enter_context(tc.tile_pool(name="pp", bufs=6))
+        tpp = ctx.enter_context(tc.psum_pool(name="tpp", bufs=2))
+        accp = ctx.enter_context(tc.psum_pool(name="accp", bufs=6))
+        if MANUAL:
+            ctx.enter_context(tc.manual_schedule())
+
+        zeros = keep.tile([P, 1], F32, name="zeros")
+        nc.vector.memset(zeros[:], 0.0)
+        junk = keep.tile([P, 1], F32, name="junk")
+        nc.scalar.activation(out=junk[:], in_=zeros[:], func=ACT.Sigmoid)
+        ident = keep.tile([P, P], F32, name="ident")
+        make_identity(nc, ident[:])
+
+        units = ((x, 0), (h_prev_dim0, 0), (h_prev_dim0, 1), (h_prev_dim1, 0), (h_prev_dim1, 1))
+        raw = []
+        for u in range(5):
+            raw.append(keep.tile([P, 4, N], BF16, name="raw%d" % u))
+        whr = []
+        wir = []
+        ctr = [[], []]
+        for i in range(4):
+            whr.append(keep.tile([P, 2, OUT_C], BF16, name="whr%d" % i))
+            wir.append(keep.tile([P, 2, IN_C], BF16, name="wir%d" % i))
+            ctr[0].append(keep.tile([P, 2, N], BF16, name="ct0r%d" % i))
+            ctr[1].append(keep.tile([P, 2, N], BF16, name="ct1r%d" % i))
+        wh_v = w_ho.rearrange("(p a) k -> p a k", a=A)
+        wi_v = w_io.rearrange("(p a) k -> p a k", a=A)
+        ct_v = (ct0.rearrange("(p a) n -> p a n", a=A), ct1.rearrange("(p a) n -> p a n", a=A))
+        bias_b = keep.tile([P, A], BF16, name="bias_b")
+        ws_b = keep.tile([P, 2], BF16, name="ws_b")
+
+        for item in LOADS:
+            kind, i = item[:-1], int(item[-1])
+            if kind == "u":
+                src, g = units[i]
+                nc.sync.dma_start(out=raw[i][:], in_=src[512 * g : 512 * (g + 1), :].rearrange("(p j) n -> p j n", j=4))
+            elif kind == "wh":
+                nc.sync.dma_start(out=whr[i][:], in_=wh_v[:, 2 * i : 2 * i + 2, :])
+            elif kind == "wi":
+                nc.sync.dma_start(out=wir[i][:], in_=wi_v[:, 2 * i : 2 * i + 2, :])
+            elif kind == "c0_":
+                nc.sync.dma_start(out=ctr[0][i][:], in_=ct_v[0][:, 2 * i : 2 * i + 2, :])
+            elif kind == "c1_":
+                nc.sync.dma_start(out=ctr[1][i][:], in_=ct_v[1][:, 2 * i : 2 * i + 2, :])
+            else:
+                nc.sync.dma_start(out=bias_b[:], in_=b_o.rearrange("(p a) o -> p (a o)", a=A))
+                nc.sync.dma_start(out=ws_b[:], in_=weighted_sum.partition_broadcast(P))
+        bias = keep.tile([P, A], F32, name="bias")
+        nc.gpsimd.tensor_copy(out=bias[:], in_=bias_b[:])
+        ws = keep.tile([P, 2], F32, name="ws")
+        nc.gpsimd.tensor_copy(out=ws[:], in_=ws_b[:])
+
+        grp = {}
+        mc = {}
+        tps = {}
+        wgs = {}
+        wcodes = {}
+        ths = {}
+        accs = {}
+        gates = {}
+        prods = {}
+        out_sb = keep.tile([P, A * N + 8], F32, name="out_sb")
+        out0_v = out_0.rearrange("(p a) n -> p a n", a=A)
+        out1_v = out_1.rearrange("(p a) n -> p (a n)", a=A)
+        pmax = keep.tile([P, 1], F32, name="pmax")
+
+        def get_grp(u):
+            if u not in grp:
+                grp[u] = keep.tile([P, N, 4], BF16, name="grp%d" % u, align_bytes=64)
+            return grp[u]
+
+        def get_wg(kind, i):
+            key = (kind, i)
+            if key not in wgs:
+                width = 2048 if kind == "H" else 1024
+                wgs[key] = keep.tile([P, width], BF16, name="wg%s%d" % (kind, i), align_bytes=64)
+            return wgs[key]
+
+        for item in ORDER:
+            parts = item.split("_")
+            kind = parts[0]
+            v = [int(s) for s in parts[1:]]
+            if kind == "ILV":
+                u = v[0]
+                nc.vector.tensor_copy(out=get_grp(u)[:, 0:NV, :], in_=raw[u][:, :, 0:NV].rearrange("p j n -> p n j"))
+            elif kind == "ILS":
+                u = v[0]
+                nc.scalar.copy(out=get_grp(u)[:, NV:N, :], in_=raw[u][:, :, NV:N].rearrange("p j n -> p n j"))
+            elif kind == "QU":
+                u = v[0]
+                codes = keep.tile([P, N], U32, name="mc%d" % u, align_bytes=64)
+                scl = keep.tile([P, N], U8, name="ms%d" % u, align_bytes=64)
+                nc.vector.quantize_mx(
+                    out=codes[:].bitcast(FP8X4), scales=scl[:], in_=get_grp(u)[:].rearrange("p n j -> p (n j)")
+                )
+                mc[u] = (codes, scl)
+            elif kind in ("TH", "TI"):
+                j = v[0]
+                tp = tpp.tile([P, 2, 2, P], F32, name="tp%s%d" % (kind, j), tag="tp")
+                for n in range(2):
+                    if kind == "TH":
+                        words, g = whr[j // 2][:, j % 2, :].bitcast(F32), n
+                    else:
+                        words, g = wir[j][:, n, :].bitcast(F32), 0
+                    for u in range(2):
+                        nc.tensor.transpose(tp[:, n, u, :], words[:, 256 * g + u : 256 * (g + 1) : 2], ident[:])
+                tps[(kind, j)] = tp
+            elif kind in ("WCH", "WCI"):
+                j = v[0]
+                if kind == "WCH":
+                    half = get_wg("H", j // 2)[:, 1024 * (j % 2) : 1024 * (j % 2 + 1)]
+                    tp = tps[("TH", j)]
+                else:
+                    half = get_wg("I", j)[:]
+                    tp = tps[("TI", j)]
+                dst = half.bitcast(F32).rearrange("p (n r u) -> p n r u", n=2, u=2)
+                src = tp[:].rearrange("p n u r -> p n r u")
+                if item in WC_ON_VECTOR:
+                    nc.vector.tensor_copy(out=dst, in_=src)
+                else:
+                    nc.scalar.copy(out=dst, in_=src)
+            elif kind in ("QWH", "QWI"):
+                i = v[0]
+                wg = get_wg(kind[2], i)
+                width = 512 if kind == "QWH" else 256
+                codes = keep.tile([P, width], U32, name="wc%s%d" % (kind, i), align_bytes=64)
+                scl = keep.tile([P, width], U8, name="wsc%s%d" % (kind, i), align_bytes=64)
+                nc.vector.quantize_mx(out=codes[:].bitcast(FP8X4), scales=scl[:], in_=wg[:])
+                wcodes[(kind[2], i)] = (codes, scl)
+            elif kind == "TANH":
+                i, dd = v
+                th = keep.tile([P, 2, N], F32, name="th%d_%d" % (i, dd))
+                nc.scalar.activation(out=th[:], in_=ctr[dd][i][:], func=ACT.Tanh)
+                ths[(i, dd)] = th
+            elif kind == "MM":
+                a, dd = v
+                i, al = a // 2, a % 2
+                acc = accp.tile([P, N], F32, name="acc%d_%d" % (a, dd), tag="acc")
+                passes = (("I", al, 0), ("H", 2 * al, 1 + 2 * dd), ("H", 2 * al + 1, 2 + 2 * dd))
+                for s, (wk, n, u) in enumerate(passes):
+                    codes, scl = wcodes[(wk, i)]
+                    nc.tensor.matmul_mx(
+                        out=acc[:],
+                        lhsT=codes[:, n * P : (n + 1) * P].bitcast(FP8X4),
+                        lhsT_scale=scl[:, n * P : (n + 1) * P],
+                        rhs=mc[u][0][:].bitcast(FP8X4),
+                        rhs_scale=mc[u][1][:],
+                        start=(s == 0),
+                        stop=(s == 2),
+                    )
+                accs[(a, dd)] = acc
+            elif kind == "SG":
+                a, dd = v
+                gate = op.tile([P, N], F32, name="o%d_%d" % (a, dd), tag="o")
+                nc.scalar.activation(
+                    out=gate[:], in_=accs[(a, dd)][:], func=ACT.Sigmoid, bias=bias[:, a : a + 1], scale=1.0
+                )
+                gates[(a, dd)] = gate
+            elif kind == "ST":
+                a, dd = v
+                pr = pp.tile([P, N], F32, name="p%d_%d" % (a, dd), tag="p")
+                nc.vector.scalar_tensor_tensor(
+                    out=pr[:], in0=gates[(a, dd)][:], scalar=ws[:, dd : dd + 1], in1=ths[(a // 2, dd)][:, a % 2, :],
+                    op0=ALU.mult, op1=ALU.mult,
+                )
+                prods[(a, dd)] = pr
+            elif kind == "AD":
+                a = v[0]
+                cols = slice(a * N, (a + 1) * N)
+                nc.vector.tensor_tensor(out=out_sb[:, cols], in0=prods[(a, 0)][:], in1=prods[(a, 1)][:], op=ALU.add)
+                nc.sync.dma_start(out=out0_v[:, a, :], in_=out_sb[:, cols])
+            elif kind == "RD":
+                a = v[0]
+                if a < A - 1:
+                    nc.vector.tensor_reduce(
+                        out=out_sb[:, A * N + a : A * N + a + 1], in_=out_sb[:, a * N : (a + 1) * N], axis=AX.X,
+                        op=ALU.max, apply_absolute_value=True,
+                    )
+                else:
+                    nc.vector.tensor_reduce(
+                        out=pmax[:], in_=out_sb[:, a * N : A * N + A - 1], axis=AX.X, op=ALU.max,
+                        apply_absolute_value=True,
+                    )
+
+        pt = tpp.tile([P, P], F32, name="pt", tag="tp")
+        nc.tensor.transpose(pt[:], pmax[:, 0:1].to_broadcast([P, P]), ident[:])
+        amax = keep.tile([P, 1], F32, name="amax")
+        nc.vector.tensor_reduce(out=amax[:], in_=pt[:], axis=AX.X, op=ALU.max)
+        rec = keep.tile([P, 1], F32, name="rec")
+        nc.vector.reciprocal(out=rec[:], in_=amax[:])
+        fac = keep.tile([P, 1], F32, name="fac")
+        nc.vector.tensor_scalar(out=fac[:], in0=rec[:], scalar1=448.0, scalar2=None, op0=ALU.mult)
+
+        for eng, c0, c1 in CASTS:
+            f8 = keep.tile([P, c1 - c0], FP8, name="f8_%d" % c0)
+            if eng == "v":
+                nc.vector.tensor_scalar(
+                    out=f8[:], in0=out_sb[:, c0:c1], scalar1=fac[:, 0:1], scalar2=None, op0=ALU.mult, saturate=False
+                )
+            else:
+                nc.scalar.activation(
+                    out=f8[:], in_=out_sb[:, c0:c1], func=ACT.Identity, scale=fac[:, 0:1], bias=zeros[:, 0:1],
+                    saturate=False,
+                )
+            nc.sync.dma_start(out=out1_v[:, c0:c1], in_=f8[:].bitcast(U8))

@@ -117,10 +117,16 @@ def tile_mdlstmcellweights_pb_kernel(
             v = [int(s) for s in parts[1:]]
             if kind == "ILV":
                 u = v[0]
-                nc.vector.tensor_copy(out=get_grp(u)[:, 0:NV, :], in_=raw[u][:, :, 0:NV].rearrange("p j n -> p n j"))
+                nc.vector.tensor_copy(
+                    out=get_grp(u)[:, 0:NV, :].rearrange("p (c i) t -> p c t i", i=4),
+                    in_=raw[u][:, :, 0:NV].rearrange("p t (c i) -> p c t i", i=4),
+                )
             elif kind == "ILS":
                 u = v[0]
-                nc.scalar.copy(out=get_grp(u)[:, NV:N, :], in_=raw[u][:, :, NV:N].rearrange("p j n -> p n j"))
+                nc.scalar.copy(
+                    out=get_grp(u)[:, NV:N, :].rearrange("p (c i) t -> p c t i", i=4),
+                    in_=raw[u][:, :, NV:N].rearrange("p t (c i) -> p c t i", i=4),
+                )
             elif kind == "QU":
                 u = v[0]
                 codes = keep.tile([P, N], U32, name="mc%d" % u, align_bytes=64)

@@ -17,13 +17,13 @@ ALU = mybir.AluOpType
 AX = mybir.AxisListType
 
 P = 128
-A = OUT_C // P
-NV = 400
-WC_ON_VECTOR = ()
-CASTS = (("v", 0, 1024), ("s", 2752, 3424), ("v", 1024, 2048), ("s", 3424, 4096), ("v", 2048, 2752))
-LOADS = ("u0", "wh0", "u1", "wi0", "u2", "c0_0", "sm0", "u3", "u4", "c1_0", "wh1", "wi1", "c0_1", "c1_1", "wh2", "wi2", "c0_2", "c1_2", "wh3", "wi3", "c0_3", "c1_3")
-ORDER = ("ILV_0", "ILS_0", "TH_0", "QU_0", "TH_1", "WCH_0", "ILV_1", "ILS_1", "TI_0", "WCH_1", "QU_1", "WCI_0", "ILV_2", "ILS_2", "TANH_0_0", "QWI_0", "QWH_0", "ILS_3", "QU_2", "ILS_4", "ILV_3", "MM_0_0", "TANH_0_1", "MM_1_0", "ILV_4", "SG_0_0", "TH_2", "SG_1_0", "QU_3", "TH_3", "WCH_2", "QU_4", "WCH_3", "TI_1", "ST_0_0", "TANH_1_0", "TH_4", "QWH_1", "MM_0_1", "ST_1_0", "WCI_1", "WCH_4", "MM_1_1", "QWI_1", "SG_0_1", "TH_5", "SG_1_1", "ST_0_1", "TI_2", "WCH_5", "ST_1_1", "MM_2_0", "WCI_2", "AD_0", "TANH_1_1", "TH_6", "AD_1", "TH_7", "RD_0", "SG_2_0", "RD_1", "MM_3_0", "WCH_6", "QWI_2", "MM_2_1", "QWH_2", "SG_3_0", "ST_2_0", "WCH_7", "TI_3", "ST_3_0", "SG_2_1", "MM_3_1", "QWH_3", "WCI_3", "MM_4_0", "ST_2_1", "SG_3_1", "QWI_3", "TANH_2_0", "MM_5_0", "AD_2", "ST_3_1", "MM_4_1", "SG_4_0", "RD_2", "SG_5_0", "MM_5_1", "AD_3", "TANH_2_1", "ST_4_0", "MM_6_0", "RD_3", "SG_4_1", "MM_7_0", "ST_5_0", "SG_5_1", "ST_4_1", "MM_6_1", "TANH_3_0", "ST_5_1", "MM_7_1", "AD_4", "SG_6_0", "AD_5", "SG_7_0", "RD_4", "TANH_3_1", "RD_5", "ST_6_0", "SG_6_1", "ST_7_0", "SG_7_1", "ST_6_1", "ST_7_1", "AD_6", "AD_7", "RD_6", "RD_7")
-MANUAL = True
+PACK = 4
+K_PASS = P * PACK
+TILES = OUT_C // P
+PAIRS = TILES // 2
+UNITS = 5
+N_VECTOR = 384
+CASTS = (("vector", 0, 1024), ("scalar", 2752, 3424), ("vector", 1024, 2048), ("scalar", 3424, 4096), ("vector", 2048, 2752))
 
 
 def tile_mdlstmcellweights_pb_kernel(
@@ -32,215 +32,268 @@ def tile_mdlstmcellweights_pb_kernel(
     nc = tc.nc
     with ExitStack() as ctx:
         keep = ctx.enter_context(tc.tile_pool(name="keep", bufs=1))
-        op = ctx.enter_context(tc.tile_pool(name="op", bufs=6))
-        pp = ctx.enter_context(tc.tile_pool(name="pp", bufs=6))
-        tpp = ctx.enter_context(tc.psum_pool(name="tpp", bufs=2))
-        accp = ctx.enter_context(tc.psum_pool(name="accp", bufs=6))
-        if MANUAL:
-            ctx.enter_context(tc.manual_schedule())
+        gate_pool = ctx.enter_context(tc.tile_pool(name="gate_pool", bufs=6))
+        prod_pool = ctx.enter_context(tc.tile_pool(name="prod_pool", bufs=6))
+        turn_pool = ctx.enter_context(tc.psum_pool(name="turn_pool", bufs=3))
+        acc_pool = ctx.enter_context(tc.psum_pool(name="acc_pool", bufs=5))
+        ctx.enter_context(tc.manual_schedule())
 
         zeros = keep.tile([P, 1], F32, name="zeros")
         nc.vector.memset(zeros[:], 0.0)
-        junk = keep.tile([P, 1], F32, name="junk")
-        nc.scalar.activation(out=junk[:], in_=zeros[:], func=ACT.Sigmoid)
+        first_act = keep.tile([P, 1], F32, name="first_act")
+        nc.scalar.activation(out=first_act[:], in_=zeros[:], func=ACT.Sigmoid)
         ident = keep.tile([P, P], F32, name="ident")
         make_identity(nc, ident[:])
 
-        units = ((x, 0), (h_prev_dim0, 0), (h_prev_dim0, 1), (h_prev_dim1, 0), (h_prev_dim1, 1))
-        raw = []
-        for u in range(5):
-            raw.append(keep.tile([P, 4, N], BF16, name="raw%d" % u))
-        whr = []
-        wir = []
-        ctr = [[], []]
-        for i in range(4):
-            whr.append(keep.tile([P, 2, OUT_C], BF16, name="whr%d" % i))
-            wir.append(keep.tile([P, 2, IN_C], BF16, name="wir%d" % i))
-            ctr[0].append(keep.tile([P, 2, N], BF16, name="ct0r%d" % i))
-            ctr[1].append(keep.tile([P, 2, N], BF16, name="ct1r%d" % i))
-        wh_v = w_ho.rearrange("(p a) k -> p a k", a=A)
-        wi_v = w_io.rearrange("(p a) k -> p a k", a=A)
-        ct_v = (ct0.rearrange("(p a) n -> p a n", a=A), ct1.rearrange("(p a) n -> p a n", a=A))
-        bias_b = keep.tile([P, A], BF16, name="bias_b")
-        ws_b = keep.tile([P, 2], BF16, name="ws_b")
+        unit_src = ((x, 0), (h_prev_dim0, 0), (h_prev_dim0, 1), (h_prev_dim1, 0), (h_prev_dim1, 1))
+        raw = [keep.tile([P, PACK, N], BF16, name="raw%d" % u) for u in range(UNITS)]
+        wh_raw = [keep.tile([P, 2, OUT_C], BF16, name="wh_raw%d" % i) for i in range(PAIRS)]
+        wi_raw = [keep.tile([P, 2, IN_C], BF16, name="wi_raw%d" % i) for i in range(PAIRS)]
+        ct_raw = [[keep.tile([P, 2, N], BF16, name="ct%d_raw%d" % (d, i)) for i in range(PAIRS)] for d in range(2)]
+        bias_bf = keep.tile([P, TILES], BF16, name="bias_bf")
+        ws_bf = keep.tile([P, 2], BF16, name="ws_bf")
+        wh_view = w_ho.rearrange("(p a) k -> p a k", a=TILES)
+        wi_view = w_io.rearrange("(p a) k -> p a k", a=TILES)
+        ct_view = (ct0.rearrange("(p a) n -> p a n", a=TILES), ct1.rearrange("(p a) n -> p a n", a=TILES))
 
-        for item in LOADS:
-            kind, i = item[:-1], int(item[-1])
-            if kind == "u":
-                src, g = units[i]
-                nc.sync.dma_start(out=raw[i][:], in_=src[512 * g : 512 * (g + 1), :].rearrange("(p j) n -> p j n", j=4))
-            elif kind == "wh":
-                nc.sync.dma_start(out=whr[i][:], in_=wh_v[:, 2 * i : 2 * i + 2, :])
-            elif kind == "wi":
-                nc.sync.dma_start(out=wir[i][:], in_=wi_v[:, 2 * i : 2 * i + 2, :])
-            elif kind == "c0_":
-                nc.sync.dma_start(out=ctr[0][i][:], in_=ct_v[0][:, 2 * i : 2 * i + 2, :])
-            elif kind == "c1_":
-                nc.sync.dma_start(out=ctr[1][i][:], in_=ct_v[1][:, 2 * i : 2 * i + 2, :])
-            else:
-                nc.sync.dma_start(out=bias_b[:], in_=b_o.rearrange("(p a) o -> p (a o)", a=A))
-                nc.sync.dma_start(out=ws_b[:], in_=weighted_sum.partition_broadcast(P))
-        bias = keep.tile([P, A], F32, name="bias")
-        nc.gpsimd.tensor_copy(out=bias[:], in_=bias_b[:])
+        def load_unit(u):
+            src, g = unit_src[u]
+            rows = src[K_PASS * g : K_PASS * (g + 1), :]
+            nc.sync.dma_start(out=raw[u][:], in_=rows.rearrange("(p j) n -> p j n", j=PACK))
+
+        def load_wh(i):
+            nc.sync.dma_start(out=wh_raw[i][:], in_=wh_view[:, 2 * i : 2 * i + 2, :])
+
+        def load_wi(i):
+            nc.sync.dma_start(out=wi_raw[i][:], in_=wi_view[:, 2 * i : 2 * i + 2, :])
+
+        def load_ct(d, i):
+            nc.sync.dma_start(out=ct_raw[d][i][:], in_=ct_view[d][:, 2 * i : 2 * i + 2, :])
+
+        load_unit(0)
+        load_unit(1)
+        load_wh(0)
+        load_unit(2)
+        load_wi(0)
+        load_unit(3)
+        load_ct(0, 0)
+        nc.sync.dma_start(out=bias_bf[:], in_=b_o.rearrange("(p a) o -> p (a o)", a=TILES))
+        nc.sync.dma_start(out=ws_bf[:], in_=weighted_sum.partition_broadcast(P))
+        load_unit(4)
+        load_ct(1, 0)
+        for i in range(1, PAIRS):
+            load_wh(i)
+            load_wi(i)
+            load_ct(0, i)
+            load_ct(1, i)
+        bias = keep.tile([P, TILES], F32, name="bias")
+        nc.gpsimd.tensor_copy(out=bias[:], in_=bias_bf[:])
         ws = keep.tile([P, 2], F32, name="ws")
-        nc.gpsimd.tensor_copy(out=ws[:], in_=ws_b[:])
+        nc.gpsimd.tensor_copy(out=ws[:], in_=ws_bf[:])
 
-        grp = {}
-        mc = {}
-        tps = {}
-        wgs = {}
-        wcodes = {}
-        ths = {}
-        accs = {}
-        gates = {}
-        prods = {}
-        out_sb = keep.tile([P, A * N + 8], F32, name="out_sb")
-        out0_v = out_0.rearrange("(p a) n -> p a n", a=A)
-        out1_v = out_1.rearrange("(p a) n -> p (a n)", a=A)
-        pmax = keep.tile([P, 1], F32, name="pmax")
+        grouped = [keep.tile([P, N, PACK], BF16, name="grouped%d" % u, align_bytes=64) for u in range(UNITS)]
+        unit_codes = [keep.tile([P, N], U32, name="unit_codes%d" % u, align_bytes=64) for u in range(UNITS)]
+        unit_scales = [keep.tile([P, N], U8, name="unit_scales%d" % u, align_bytes=64) for u in range(UNITS)]
 
-        def get_grp(u):
-            if u not in grp:
-                grp[u] = keep.tile([P, N, 4], BF16, name="grp%d" % u, align_bytes=64)
-            return grp[u]
+        def interleave(u):
+            nc.vector.tensor_copy(
+                out=grouped[u][:, 0:N_VECTOR, :], in_=raw[u][:, :, 0:N_VECTOR].rearrange("p j n -> p n j")
+            )
+            nc.scalar.copy(out=grouped[u][:, N_VECTOR:N, :], in_=raw[u][:, :, N_VECTOR:N].rearrange("p j n -> p n j"))
 
-        def get_wg(kind, i):
-            key = (kind, i)
-            if key not in wgs:
-                width = 2048 if kind == "H" else 1024
-                wgs[key] = keep.tile([P, width], BF16, name="wg%s%d" % (kind, i), align_bytes=64)
-            return wgs[key]
+        def quantize_unit(u):
+            nc.vector.quantize_mx(
+                out=unit_codes[u][:].bitcast(FP8X4),
+                scales=unit_scales[u][:],
+                in_=grouped[u][:].rearrange("p n j -> p (n j)"),
+            )
 
-        for item in ORDER:
-            parts = item.split("_")
-            kind = parts[0]
-            v = [int(s) for s in parts[1:]]
-            if kind == "ILV":
-                u = v[0]
-                nc.vector.tensor_copy(
-                    out=get_grp(u)[:, 0:NV, :].rearrange("p (c i) t -> p c t i", i=4),
-                    in_=raw[u][:, :, 0:NV].rearrange("p t (c i) -> p c t i", i=4),
+        def warm(u):
+            idle_sum = acc_pool.tile([P, N], F32, name="idle_sum%d" % u, tag="acc")
+            for j in range(2):
+                nc.tensor.matmul(out=idle_sum[:], lhsT=raw[u][:, j, 0:P], rhs=raw[u][:, 2 + j, :], start=True, stop=True)
+
+        wh_grouped = [keep.tile([P, 4 * K_PASS], BF16, name="wh_grouped%d" % i, align_bytes=64) for i in range(PAIRS)]
+        wi_grouped = [keep.tile([P, 2 * K_PASS], BF16, name="wi_grouped%d" % i, align_bytes=64) for i in range(PAIRS)]
+        wh_codes = [keep.tile([P, 4 * P], U32, name="wh_codes%d" % i, align_bytes=64) for i in range(PAIRS)]
+        wh_scales = [keep.tile([P, 4 * P], U8, name="wh_scales%d" % i, align_bytes=64) for i in range(PAIRS)]
+        wi_codes = [keep.tile([P, 2 * P], U32, name="wi_codes%d" % i, align_bytes=64) for i in range(PAIRS)]
+        wi_scales = [keep.tile([P, 2 * P], U8, name="wi_scales%d" % i, align_bytes=64) for i in range(PAIRS)]
+        turned = {}
+
+        def turn(name, sources):
+            bank = turn_pool.tile([P, 2, 2, P], F32, name="turned_%s" % name, tag="turned")
+            for s, (rows, g) in enumerate(sources):
+                words = rows.bitcast(F32)
+                for u in range(2):
+                    nc.tensor.transpose(bank[:, s, u, :], words[:, 256 * g + u : 256 * (g + 1) : 2], ident[:])
+            turned[name] = bank
+
+        def turn_wh(a):
+            rows = wh_raw[a // 2][:, a % 2, :]
+            turn("h%d" % a, ((rows, 0), (rows, 1)))
+
+        def turn_wi(i):
+            turn("i%d" % i, ((wi_raw[i][:, 0, :], 0), (wi_raw[i][:, 1, :], 0)))
+
+        def turn_pair(i):
+            turn_wh(2 * i)
+            turn_wh(2 * i + 1)
+            turn_wi(i)
+
+        def copy_out(engine, name, dst):
+            out = dst.bitcast(F32).rearrange("p (s r u) -> p s r u", s=2, u=2)
+            in_ = turned[name][:].rearrange("p s u r -> p s r u")
+            if engine == "vector":
+                nc.vector.tensor_copy(out=out, in_=in_)
+            else:
+                nc.scalar.copy(out=out, in_=in_)
+
+        def copy_wh(a):
+            copy_out("scalar", "h%d" % a, wh_grouped[a // 2][:, 2 * K_PASS * (a % 2) : 2 * K_PASS * (a % 2 + 1)])
+
+        def copy_wi(engine, i):
+            copy_out(engine, "i%d" % i, wi_grouped[i][:])
+
+        def quantize_pair(i):
+            nc.vector.quantize_mx(out=wh_codes[i][:].bitcast(FP8X4), scales=wh_scales[i][:], in_=wh_grouped[i][:])
+            nc.vector.quantize_mx(out=wi_codes[i][:].bitcast(FP8X4), scales=wi_scales[i][:], in_=wi_grouped[i][:])
+
+        tanh_c = {}
+        acc = {}
+        gate = {}
+        prod = {}
+        out_sb = keep.tile([P, TILES * N + 8], F32, name="out_sb")
+        out0_view = out_0.rearrange("(p a) n -> p a n", a=TILES)
+        out1_view = out_1.rearrange("(p a) n -> p (a n)", a=TILES)
+        part_max = keep.tile([P, 1], F32, name="part_max")
+
+        def tanh_pair(i, d):
+            tanh_c[(i, d)] = keep.tile([P, 2, N], F32, name="tanh_c%d_%d" % (i, d))
+            nc.scalar.activation(out=tanh_c[(i, d)][:], in_=ct_raw[d][i][:], func=ACT.Tanh)
+
+        def matmuls(i, d):
+            for a in (2 * i, 2 * i + 1):
+                acc[(a, d)] = acc_pool.tile([P, N], F32, name="acc%d_%d" % (a, d), tag="acc")
+                half = a % 2
+                passes = (
+                    (wi_codes[i], wi_scales[i], half, 0),
+                    (wh_codes[i], wh_scales[i], 2 * half, 1 + 2 * d),
+                    (wh_codes[i], wh_scales[i], 2 * half + 1, 2 + 2 * d),
                 )
-            elif kind == "ILS":
-                u = v[0]
-                nc.scalar.copy(
-                    out=get_grp(u)[:, NV:N, :].rearrange("p (c i) t -> p c t i", i=4),
-                    in_=raw[u][:, :, NV:N].rearrange("p t (c i) -> p c t i", i=4),
-                )
-            elif kind == "QU":
-                u = v[0]
-                codes = keep.tile([P, N], U32, name="mc%d" % u, align_bytes=64)
-                scl = keep.tile([P, N], U8, name="ms%d" % u, align_bytes=64)
-                nc.vector.quantize_mx(
-                    out=codes[:].bitcast(FP8X4), scales=scl[:], in_=get_grp(u)[:].rearrange("p n j -> p (n j)")
-                )
-                mc[u] = (codes, scl)
-            elif kind in ("TH", "TI"):
-                j = v[0]
-                tp = tpp.tile([P, 2, 2, P], F32, name="tp%s%d" % (kind, j), tag="tp")
-                for n in range(2):
-                    if kind == "TH":
-                        words, g = whr[j // 2][:, j % 2, :].bitcast(F32), n
-                    else:
-                        words, g = wir[j][:, n, :].bitcast(F32), 0
-                    for u in range(2):
-                        nc.tensor.transpose(tp[:, n, u, :], words[:, 256 * g + u : 256 * (g + 1) : 2], ident[:])
-                tps[(kind, j)] = tp
-            elif kind in ("WCH", "WCI"):
-                j = v[0]
-                if kind == "WCH":
-                    half = get_wg("H", j // 2)[:, 1024 * (j % 2) : 1024 * (j % 2 + 1)]
-                    tp = tps[("TH", j)]
-                else:
-                    half = get_wg("I", j)[:]
-                    tp = tps[("TI", j)]
-                dst = half.bitcast(F32).rearrange("p (n r u) -> p n r u", n=2, u=2)
-                src = tp[:].rearrange("p n u r -> p n r u")
-                if item in WC_ON_VECTOR:
-                    nc.vector.tensor_copy(out=dst, in_=src)
-                else:
-                    nc.scalar.copy(out=dst, in_=src)
-            elif kind in ("QWH", "QWI"):
-                i = v[0]
-                wg = get_wg(kind[2], i)
-                width = 512 if kind == "QWH" else 256
-                codes = keep.tile([P, width], U32, name="wc%s%d" % (kind, i), align_bytes=64)
-                scl = keep.tile([P, width], U8, name="wsc%s%d" % (kind, i), align_bytes=64)
-                nc.vector.quantize_mx(out=codes[:].bitcast(FP8X4), scales=scl[:], in_=wg[:])
-                wcodes[(kind[2], i)] = (codes, scl)
-            elif kind == "TANH":
-                i, dd = v
-                th = keep.tile([P, 2, N], F32, name="th%d_%d" % (i, dd))
-                nc.scalar.activation(out=th[:], in_=ctr[dd][i][:], func=ACT.Tanh)
-                ths[(i, dd)] = th
-            elif kind == "MM":
-                a, dd = v
-                i, al = a // 2, a % 2
-                acc = accp.tile([P, N], F32, name="acc%d_%d" % (a, dd), tag="acc")
-                passes = (("I", al, 0), ("H", 2 * al, 1 + 2 * dd), ("H", 2 * al + 1, 2 + 2 * dd))
-                for s, (wk, n, u) in enumerate(passes):
-                    codes, scl = wcodes[(wk, i)]
+                for s, (codes, scales, c, u) in enumerate(passes):
                     nc.tensor.matmul_mx(
-                        out=acc[:],
-                        lhsT=codes[:, n * P : (n + 1) * P].bitcast(FP8X4),
-                        lhsT_scale=scl[:, n * P : (n + 1) * P],
-                        rhs=mc[u][0][:].bitcast(FP8X4),
-                        rhs_scale=mc[u][1][:],
+                        out=acc[(a, d)][:],
+                        lhsT=codes[:, c * P : (c + 1) * P].bitcast(FP8X4),
+                        lhsT_scale=scales[:, c * P : (c + 1) * P],
+                        rhs=unit_codes[u][:].bitcast(FP8X4),
+                        rhs_scale=unit_scales[u][:],
                         start=(s == 0),
                         stop=(s == 2),
                     )
-                accs[(a, dd)] = acc
-            elif kind == "SG":
-                a, dd = v
-                gate = op.tile([P, N], F32, name="o%d_%d" % (a, dd), tag="o")
+
+        def gates(i, d):
+            for a in (2 * i, 2 * i + 1):
+                gate[(a, d)] = gate_pool.tile([P, N], F32, name="gate%d_%d" % (a, d), tag="gate")
                 nc.scalar.activation(
-                    out=gate[:], in_=accs[(a, dd)][:], func=ACT.Sigmoid, bias=bias[:, a : a + 1], scale=1.0
+                    out=gate[(a, d)][:], in_=acc[(a, d)][:], func=ACT.Sigmoid, bias=bias[:, a : a + 1], scale=1.0
                 )
-                gates[(a, dd)] = gate
-            elif kind == "ST":
-                a, dd = v
-                pr = pp.tile([P, N], F32, name="p%d_%d" % (a, dd), tag="p")
+
+        def products(i, d):
+            for a in (2 * i, 2 * i + 1):
+                prod[(a, d)] = prod_pool.tile([P, N], F32, name="prod%d_%d" % (a, d), tag="prod")
                 nc.vector.scalar_tensor_tensor(
-                    out=pr[:], in0=gates[(a, dd)][:], scalar=ws[:, dd : dd + 1], in1=ths[(a // 2, dd)][:, a % 2, :],
+                    out=prod[(a, d)][:], in0=gate[(a, d)][:], scalar=ws[:, d : d + 1], in1=tanh_c[(i, d)][:, a % 2, :],
                     op0=ALU.mult, op1=ALU.mult,
                 )
-                prods[(a, dd)] = pr
-            elif kind == "AD":
-                a = v[0]
+
+        def sums(i):
+            for a in (2 * i, 2 * i + 1):
                 cols = slice(a * N, (a + 1) * N)
-                nc.vector.tensor_tensor(out=out_sb[:, cols], in0=prods[(a, 0)][:], in1=prods[(a, 1)][:], op=ALU.add)
-                nc.sync.dma_start(out=out0_v[:, a, :], in_=out_sb[:, cols])
-            elif kind == "RD":
-                a = v[0]
-                if a < A - 1:
+                nc.vector.tensor_tensor(out=out_sb[:, cols], in0=prod[(a, 0)][:], in1=prod[(a, 1)][:], op=ALU.add)
+                nc.sync.dma_start(out=out0_view[:, a, :], in_=out_sb[:, cols])
+
+        def maxima(i):
+            for a in (2 * i, 2 * i + 1):
+                if a < TILES - 1:
                     nc.vector.tensor_reduce(
-                        out=out_sb[:, A * N + a : A * N + a + 1], in_=out_sb[:, a * N : (a + 1) * N], axis=AX.X,
-                        op=ALU.max, apply_absolute_value=True,
+                        out=out_sb[:, TILES * N + a : TILES * N + a + 1], in_=out_sb[:, a * N : (a + 1) * N],
+                        axis=AX.X, op=ALU.max, apply_absolute_value=True,
                     )
                 else:
                     nc.vector.tensor_reduce(
-                        out=pmax[:], in_=out_sb[:, a * N : A * N + A - 1], axis=AX.X, op=ALU.max,
-                        apply_absolute_value=True,
+                        out=part_max[:], in_=out_sb[:, a * N : TILES * N + TILES - 1],
+                        axis=AX.X, op=ALU.max, apply_absolute_value=True,
                     )
 
-        pt = tpp.tile([P, P], F32, name="pt", tag="tp")
-        nc.tensor.transpose(pt[:], pmax[:, 0:1].to_broadcast([P, P]), ident[:])
-        amax = keep.tile([P, 1], F32, name="amax")
-        nc.vector.tensor_reduce(out=amax[:], in_=pt[:], axis=AX.X, op=ALU.max)
-        rec = keep.tile([P, 1], F32, name="rec")
-        nc.vector.reciprocal(out=rec[:], in_=amax[:])
-        fac = keep.tile([P, 1], F32, name="fac")
-        nc.vector.tensor_scalar(out=fac[:], in0=rec[:], scalar1=448.0, scalar2=None, op0=ALU.mult)
+        interleave(0)
+        warm(0)
+        interleave(1)
+        warm(1)
+        quantize_unit(0)
+        turn_wh(0)
+        turn_wh(1)
+        warm(2)
+        turn_wi(0)
+        warm(3)
+        copy_wh(0)
+        interleave(2)
+        quantize_unit(1)
+        copy_wh(1)
+        copy_wi("scalar", 0)
+        quantize_unit(2)
+        quantize_pair(0)
+        matmuls(0, 0)
+        interleave(3)
+        tanh_pair(0, 0)
+        interleave(4)
+        quantize_unit(3)
+        tanh_pair(0, 1)
+        quantize_unit(4)
 
-        for eng, c0, c1 in CASTS:
-            f8 = keep.tile([P, c1 - c0], FP8, name="f8_%d" % c0)
-            if eng == "v":
+        for h in range(2 * PAIRS):
+            i, d = h // 2, h % 2
+            nxt = h + 1
+            if nxt < PAIRS:
+                turn_pair(nxt)
+            if nxt < 2 * PAIRS:
+                matmuls(nxt // 2, nxt % 2)
+            gates(i, d)
+            products(i, d)
+            if d == 1:
+                sums(i)
+            elif i > 0:
+                maxima(i - 1)
+            if nxt < PAIRS:
+                copy_wh(2 * nxt)
+                copy_wh(2 * nxt + 1)
+                copy_wi("vector", nxt)
+                quantize_pair(nxt)
+            if d == 1 and i + 1 < PAIRS:
+                tanh_pair(i + 1, 0)
+                tanh_pair(i + 1, 1)
+        maxima(PAIRS - 1)
+
+        spread = turn_pool.tile([P, P], F32, name="spread", tag="turned")
+        nc.tensor.transpose(spread[:], part_max[:, 0:1].to_broadcast([P, P]), ident[:])
+        scaled = keep.tile([P, P], F32, name="scaled")
+        scale = keep.tile([P, 1], F32, name="scale")
+        nc.vector.tensor_scalar(
+            out=scaled[:], in0=spread[:], scalar1=1.0 / 448.0, scalar2=None, op0=ALU.mult, op1=ALU.max, accum_out=scale[:]
+        )
+        factor = keep.tile([P, 1], F32, name="factor")
+        nc.vector.reciprocal(out=factor[:], in_=scale[:])
+
+        for engine, c0, c1 in CASTS:
+            codes8 = keep.tile([P, c1 - c0], FP8, name="codes8_%d" % c0)
+            if engine == "vector":
                 nc.vector.tensor_scalar(
-                    out=f8[:], in0=out_sb[:, c0:c1], scalar1=fac[:, 0:1], scalar2=None, op0=ALU.mult, saturate=False
+                    out=codes8[:], in0=out_sb[:, c0:c1], scalar1=factor[:, 0:1], scalar2=None, op0=ALU.mult,
+                    saturate=False,
                 )
             else:
                 nc.scalar.activation(
-                    out=f8[:], in_=out_sb[:, c0:c1], func=ACT.Identity, scale=fac[:, 0:1], bias=zeros[:, 0:1],
+                    out=codes8[:], in_=out_sb[:, c0:c1], func=ACT.Identity, scale=factor[:, 0:1], bias=zeros[:, 0:1],
                     saturate=False,
                 )
-            nc.sync.dma_start(out=out1_v[:, c0:c1], in_=f8[:].bitcast(U8))
+            nc.sync.dma_start(out=out1_view[:, c0:c1], in_=codes8[:].bitcast(U8))

@@ -38,6 +38,11 @@ def tile_mdlstmcellweights_pb_kernel(
         acc_pool = ctx.enter_context(tc.psum_pool(name="acc_pool", bufs=5))
         ctx.enter_context(tc.manual_schedule())
 
+        bias_bf = keep.tile([P, TILES], BF16, name="bias_bf")
+        ws_bf = keep.tile([P, 2], BF16, name="ws_bf")
+        nc.scalar.dma_start(out=bias_bf[:], in_=b_o.rearrange("(p a) o -> p (a o)", a=TILES))
+        nc.scalar.dma_start(out=ws_bf[:], in_=weighted_sum.partition_broadcast(P))
+
         zeros = keep.tile([P, 1], F32, name="zeros")
         nc.vector.memset(zeros[:], 0.0)
         first_act = keep.tile([P, 1], F32, name="first_act")
@@ -50,8 +55,6 @@ def tile_mdlstmcellweights_pb_kernel(
         wh_raw = [keep.tile([P, 2, OUT_C], BF16, name="wh_raw%d" % i) for i in range(PAIRS)]
         wi_raw = [keep.tile([P, 2, IN_C], BF16, name="wi_raw%d" % i) for i in range(PAIRS)]
         ct_raw = [[keep.tile([P, 2, N], BF16, name="ct%d_raw%d" % (d, i)) for i in range(PAIRS)] for d in range(2)]
-        bias_bf = keep.tile([P, TILES], BF16, name="bias_bf")
-        ws_bf = keep.tile([P, 2], BF16, name="ws_bf")
         wh_view = w_ho.rearrange("(p a) k -> p a k", a=TILES)
         wi_view = w_io.rearrange("(p a) k -> p a k", a=TILES)
         ct_view = (ct0.rearrange("(p a) n -> p a n", a=TILES), ct1.rearrange("(p a) n -> p a n", a=TILES))
@@ -77,8 +80,6 @@ def tile_mdlstmcellweights_pb_kernel(
         load_wi(0)
         load_unit(3)
         load_ct(0, 0)
-        nc.sync.dma_start(out=bias_bf[:], in_=b_o.rearrange("(p a) o -> p (a o)", a=TILES))
-        nc.sync.dma_start(out=ws_bf[:], in_=weighted_sum.partition_broadcast(P))
         load_unit(4)
         load_ct(1, 0)
         for i in range(1, PAIRS):

@@ -81,8 +81,12 @@ def tile_mdlstmcellweights_pb_kernel(
         load_unit(3)
         load_ct(0, 0)
         load_unit(4)
+        load_wh(1)
+        load_wi(1)
         load_ct(1, 0)
-        for i in range(1, PAIRS):
+        load_ct(0, 1)
+        load_ct(1, 1)
+        for i in range(2, PAIRS):
             load_wh(i)
             load_wi(i)
             load_ct(0, i)
@@ -249,6 +253,7 @@ def tile_mdlstmcellweights_pb_kernel(
         tanh_pair(0, 0)
         interleave(4)
         quantize_unit(3)
+        gates(0, 0)
         tanh_pair(0, 1)
         quantize_unit(4)
 
@@ -259,7 +264,8 @@ def tile_mdlstmcellweights_pb_kernel(
                 turn_pair(nxt)
             if nxt < 2 * PAIRS:
                 matmuls(nxt // 2, nxt % 2)
-            gates(i, d)
+            if h > 0:
+                gates(i, d)
             products(i, d)
             if d == 1:
                 sums(i)

@@ -160,9 +160,15 @@ def tile_mdlstmcellweights_pb_kernel(
         def copy_wi(engine, i):
             copy_out(engine, "i%d" % i, wi_grouped[i][:])
 
-        def quantize_pair(i):
+        def quantize_wh(i):
             nc.vector.quantize_mx(out=wh_codes[i][:].bitcast(FP8X4), scales=wh_scales[i][:], in_=wh_grouped[i][:])
+
+        def quantize_wi(i):
             nc.vector.quantize_mx(out=wi_codes[i][:].bitcast(FP8X4), scales=wi_scales[i][:], in_=wi_grouped[i][:])
+
+        def quantize_pair(i):
+            quantize_wh(i)
+            quantize_wi(i)
 
         tanh_c = {}
         acc = {}
@@ -241,13 +247,14 @@ def tile_mdlstmcellweights_pb_kernel(
         warm(2)
         turn_wi(0)
         warm(3)
-        copy_wh(0)
-        interleave(2)
         quantize_unit(1)
+        copy_wh(0)
         copy_wh(1)
+        interleave(2)
+        quantize_wh(0)
         copy_wi("scalar", 0)
         quantize_unit(2)
-        quantize_pair(0)
+        quantize_wi(0)
         matmuls(0, 0)
         interleave(3)
         tanh_pair(0, 0)
@@ -274,11 +281,10 @@ def tile_mdlstmcellweights_pb_kernel(
             if nxt < PAIRS:
                 copy_wh(2 * nxt)
                 copy_wh(2 * nxt + 1)
-                copy_wi("vector", nxt)
+                copy_wi("vector" if nxt < PAIRS - 1 else "scalar", nxt)
                 quantize_pair(nxt)
-            if d == 1 and i + 1 < PAIRS:
-                tanh_pair(i + 1, 0)
-                tanh_pair(i + 1, 1)
+            if 2 <= nxt < 2 * PAIRS:
+                tanh_pair(nxt // 2, nxt % 2)
         maxima(PAIRS - 1)
 
         spread = turn_pool.tile([P, P], F32, name="spread", tag="turned")

@@ -75,7 +75,8 @@ def tile_mdlstmcellweights_pb_kernel(
 
         load_unit(0)
         load_unit(1)
-        load_wh(0)
+        nc.sync.dma_start(out=wh_raw[0][:, 0, :], in_=wh_view[:, 0, :])
+        nc.sync.dma_start(out=wh_raw[0][:, 1, :], in_=wh_view[:, 1, :])
         load_unit(2)
         load_wi(0)
         load_unit(3)
@@ -91,10 +92,6 @@ def tile_mdlstmcellweights_pb_kernel(
             load_wi(i)
             load_ct(0, i)
             load_ct(1, i)
-        bias = keep.tile([P, TILES], F32, name="bias")
-        nc.gpsimd.tensor_copy(out=bias[:], in_=bias_bf[:])
-        ws = keep.tile([P, 2], F32, name="ws")
-        nc.gpsimd.tensor_copy(out=ws[:], in_=ws_bf[:])
 
         grouped = [keep.tile([P, N, PACK], BF16, name="grouped%d" % u, align_bytes=64) for u in range(UNITS)]
         unit_codes = [keep.tile([P, N], U32, name="unit_codes%d" % u, align_bytes=64) for u in range(UNITS)]
@@ -207,14 +204,14 @@ def tile_mdlstmcellweights_pb_kernel(
             for a in (2 * i, 2 * i + 1):
                 gate[(a, d)] = gate_pool.tile([P, N], F32, name="gate%d_%d" % (a, d), tag="gate")
                 nc.scalar.activation(
-                    out=gate[(a, d)][:], in_=acc[(a, d)][:], func=ACT.Sigmoid, bias=bias[:, a : a + 1], scale=1.0
+                    out=gate[(a, d)][:], in_=acc[(a, d)][:], func=ACT.Sigmoid, bias=bias_bf[:, a : a + 1], scale=1.0
                 )
 
         def products(i, d):
             for a in (2 * i, 2 * i + 1):
                 prod[(a, d)] = prod_pool.tile([P, N], F32, name="prod%d_%d" % (a, d), tag="prod")
                 nc.vector.scalar_tensor_tensor(
-                    out=prod[(a, d)][:], in0=gate[(a, d)][:], scalar=ws[:, d : d + 1], in1=tanh_c[(i, d)][:, a % 2, :],
+                    out=prod[(a, d)][:], in0=gate[(a, d)][:], scalar=ws_bf[:, d : d + 1], in1=tanh_c[(i, d)][:, a % 2, :],
                     op0=ALU.mult, op1=ALU.mult,
                 )
 
@@ -225,17 +222,20 @@ def tile_mdlstmcellweights_pb_kernel(
                 nc.sync.dma_start(out=out0_view[:, a, :], in_=out_sb[:, cols])
 
         def maxima(i):
-            for a in (2 * i, 2 * i + 1):
-                if a < TILES - 1:
-                    nc.vector.tensor_reduce(
-                        out=out_sb[:, TILES * N + a : TILES * N + a + 1], in_=out_sb[:, a * N : (a + 1) * N],
-                        axis=AX.X, op=ALU.max, apply_absolute_value=True,
-                    )
-                else:
-                    nc.vector.tensor_reduce(
-                        out=part_max[:], in_=out_sb[:, a * N : TILES * N + TILES - 1],
-                        axis=AX.X, op=ALU.max, apply_absolute_value=True,
-                    )
+            if i < PAIRS - 1:
+                nc.vector.tensor_reduce(
+                    out=out_sb[:, TILES * N + i : TILES * N + i + 1], in_=out_sb[:, 2 * i * N : (2 * i + 2) * N],
+                    axis=AX.X, op=ALU.max, apply_absolute_value=True,
+                )
+            else:
+                nc.vector.tensor_reduce(
+                    out=out_sb[:, TILES * N + i : TILES * N + i + 1], in_=out_sb[:, 2 * i * N : (2 * i + 1) * N],
+                    axis=AX.X, op=ALU.max, apply_absolute_value=True,
+                )
+                nc.vector.tensor_reduce(
+                    out=part_max[:], in_=out_sb[:, (2 * i + 1) * N : TILES * N + PAIRS],
+                    axis=AX.X, op=ALU.max, apply_absolute_value=True,
+                )
 
         interleave(0)
         warm(0)
@@ -261,7 +261,6 @@ def tile_mdlstmcellweights_pb_kernel(
         interleave(4)
         quantize_unit(3)
         gates(0, 0)
-        tanh_pair(0, 1)
         quantize_unit(4)
 
         for h in range(2 * PAIRS):
@@ -283,7 +282,7 @@ def tile_mdlstmcellweights_pb_kernel(
                 copy_wh(2 * nxt + 1)
                 copy_wi("vector" if nxt < PAIRS - 1 else "scalar", nxt)
                 quantize_pair(nxt)
-            if 2 <= nxt < 2 * PAIRS:
+            if nxt < 2 * PAIRS:
                 tanh_pair(nxt // 2, nxt % 2)
         maxima(PAIRS - 1)
 

@@ -263,6 +263,15 @@ def tile_mdlstmcellweights_pb_kernel(
         gates(0, 0)
         quantize_unit(4)
 
+        late = {}
+
+        def keep_clock(fresh):
+            if not late:
+                late["sum"] = turn_pool.tile([P, P], F32, name="late_sum", tag="turned")
+            for columns in fresh:
+                for j in range(2):
+                    nc.tensor.matmul(out=late["sum"][:], lhsT=ident[:], rhs=columns, start=True, stop=True)
+
         for h in range(2 * PAIRS):
             i, d = h // 2, h % 2
             nxt = h + 1
@@ -273,6 +282,8 @@ def tile_mdlstmcellweights_pb_kernel(
             if h > 0:
                 gates(i, d)
             products(i, d)
+            if i == PAIRS - 1:
+                keep_clock([prod[(a, d)][:, 0:P] for a in (2 * i, 2 * i + 1)])
             if d == 1:
                 sums(i)
             elif i > 0:
@@ -284,6 +295,7 @@ def tile_mdlstmcellweights_pb_kernel(
                 quantize_pair(nxt)
             if nxt < 2 * PAIRS:
                 tanh_pair(nxt // 2, nxt % 2)
+        keep_clock([out_sb[:, a * N : a * N + P] for a in (TILES - 2, TILES - 1)])
         maxima(PAIRS - 1)
 
         spread = turn_pool.tile([P, P], F32, name="spread", tag="turned")

@@ -67,6 +67,10 @@ def tile_mdlstmcellweights_pb_kernel(
         def load_wh(i):
             nc.sync.dma_start(out=wh_raw[i][:], in_=wh_view[:, 2 * i : 2 * i + 2, :])
 
+        def load_wh_tiles(i):
+            for j in range(2):
+                nc.sync.dma_start(out=wh_raw[i][:, j, :], in_=wh_view[:, 2 * i + j, :])
+
         def load_wi(i):
             nc.sync.dma_start(out=wi_raw[i][:], in_=wi_view[:, 2 * i : 2 * i + 2, :])
 
@@ -75,21 +79,22 @@ def tile_mdlstmcellweights_pb_kernel(
 
         load_unit(0)
         load_unit(1)
-        nc.sync.dma_start(out=wh_raw[0][:, 0, :], in_=wh_view[:, 0, :])
-        nc.sync.dma_start(out=wh_raw[0][:, 1, :], in_=wh_view[:, 1, :])
+        load_wh_tiles(0)
         load_unit(2)
         load_wi(0)
         load_unit(3)
         load_ct(0, 0)
         load_unit(4)
-        load_wh(1)
+        load_wh_tiles(1)
         load_wi(1)
         load_ct(1, 0)
+        load_wh(2)
         load_ct(0, 1)
+        load_wi(2)
+        load_wh(3)
+        load_wi(3)
         load_ct(1, 1)
         for i in range(2, PAIRS):
-            load_wh(i)
-            load_wi(i)
             load_ct(0, i)
             load_ct(1, i)
 

@@ -22,7 +22,7 @@ K_PASS = P * PACK
 TILES = OUT_C // P
 PAIRS = TILES // 2
 UNITS = 5
-N_VECTOR = 384
+N_VECTOR = (384,384,384,384,448)
 CASTS = (("vector", 0, 1024), ("scalar", 2752, 3424), ("vector", 1024, 2048), ("scalar", 3424, 4096), ("vector", 2048, 2752))
 
 
@@ -77,13 +77,13 @@ def tile_mdlstmcellweights_pb_kernel(
         def load_ct(d, i):
             nc.sync.dma_start(out=ct_raw[d][i][:], in_=ct_view[d][:, 2 * i : 2 * i + 2, :])
 
+        load_wi(0)
         load_unit(0)
         load_unit(1)
         load_wh_tiles(0)
         load_unit(2)
-        load_wi(0)
-        load_unit(3)
         load_ct(0, 0)
+        load_unit(3)
         load_unit(4)
         load_wh_tiles(1)
         load_wi(1)
@@ -104,9 +104,9 @@ def tile_mdlstmcellweights_pb_kernel(
 
         def interleave(u):
             nc.vector.tensor_copy(
-                out=grouped[u][:, 0:N_VECTOR, :], in_=raw[u][:, :, 0:N_VECTOR].rearrange("p j n -> p n j")
+                out=grouped[u][:, 0:N_VECTOR[u], :], in_=raw[u][:, :, 0:N_VECTOR[u]].rearrange("p j n -> p n j")
             )
-            nc.scalar.copy(out=grouped[u][:, N_VECTOR:N, :], in_=raw[u][:, :, N_VECTOR:N].rearrange("p j n -> p n j"))
+            nc.scalar.copy(out=grouped[u][:, N_VECTOR[u]:N, :], in_=raw[u][:, :, N_VECTOR[u]:N].rearrange("p j n -> p n j"))
 
         def quantize_unit(u):
             nc.vector.quantize_mx(
@@ -114,6 +114,11 @@ def tile_mdlstmcellweights_pb_kernel(
                 scales=unit_scales[u][:],
                 in_=grouped[u][:].rearrange("p n j -> p (n j)"),
             )
+
+        def warm_ident(n):
+            idle_sum = acc_pool.tile([P, P], F32, name="early_sum", tag="acc")
+            for j in range(n):
+                nc.tensor.matmul(out=idle_sum[:], lhsT=ident[:], rhs=ident[:], start=True, stop=True)
 
         def warm(u):
             idle_sum = acc_pool.tile([P, N], F32, name="idle_sum%d" % u, tag="acc")
@@ -242,27 +247,27 @@ def tile_mdlstmcellweights_pb_kernel(
                     axis=AX.X, op=ALU.max, apply_absolute_value=True,
                 )
 
+        warm_ident(3)
+        turn_wi(0)
+        copy_wi("scalar", 0)
         interleave(0)
         warm(0)
+        quantize_wi(0)
         interleave(1)
         warm(1)
         quantize_unit(0)
         turn_wh(0)
         turn_wh(1)
-        warm(2)
-        turn_wi(0)
-        warm(3)
         quantize_unit(1)
         copy_wh(0)
         copy_wh(1)
         interleave(2)
+        warm(2)
         quantize_wh(0)
-        copy_wi("scalar", 0)
         quantize_unit(2)
-        quantize_wi(0)
         matmuls(0, 0)
-        interleave(3)
         tanh_pair(0, 0)
+        interleave(3)
         interleave(4)
         quantize_unit(3)
         gates(0, 0)

@@ -177,21 +177,36 @@ def tile_mdlstmcellweights_pb_kernel(
             quantize_wh(i)
             quantize_wi(i)
 
-        tanh_c = {}
         acc = {}
         gate = {}
         prod = {}
+        tile_sum = {}
         out_sb = keep.tile([P, TILES * N + 8], F32, name="out_sb")
         out0_view = out_0.rearrange("(p a) n -> p a n", a=TILES)
         out1_view = out_1.rearrange("(p a) n -> p (a n)", a=TILES)
         part_max = keep.tile([P, 1], F32, name="part_max")
 
-        def tanh_pair(i, d):
-            tanh_c[(i, d)] = keep.tile([P, 2, N], F32, name="tanh_c%d_%d" % (i, d))
-            nc.scalar.activation(out=tanh_c[(i, d)][:], in_=ct_raw[d][i][:], func=ACT.Tanh)
+        def step_items(h):
+            i, j = h // 2, h % 2
+            if i < PAIRS - 1:
+                return [(2 * i, j), (2 * i + 1, j)]
+            return [(2 * i + j, 0), (2 * i + j, 1)]
 
-        def matmuls(i, d):
-            for a in (2 * i, 2 * i + 1):
+        tanh_c = {
+            (i, d): keep.tile([P, 2, N], F32, name="tanh_c%d_%d" % (i, d)) for i in range(PAIRS) for d in range(2)
+        }
+
+        def tanh_step(h):
+            i, j = h // 2, h % 2
+            if i < PAIRS - 1:
+                nc.scalar.activation(out=tanh_c[(i, j)][:], in_=ct_raw[j][i][:], func=ACT.Tanh)
+            else:
+                for d in range(2):
+                    nc.scalar.activation(out=tanh_c[(i, d)][:, j, :], in_=ct_raw[d][i][:, j, :], func=ACT.Tanh)
+
+        def matmuls(h):
+            for a, d in step_items(h):
+                i = a // 2
                 acc[(a, d)] = acc_pool.tile([P, N], F32, name="acc%d_%d" % (a, d), tag="acc")
                 half = a % 2
                 passes = (
@@ -210,26 +225,40 @@ def tile_mdlstmcellweights_pb_kernel(
                         stop=(s == 2),
                     )
 
-        def gates(i, d):
-            for a in (2 * i, 2 * i + 1):
+        def gates(h):
+            for a, d in step_items(h):
                 gate[(a, d)] = gate_pool.tile([P, N], F32, name="gate%d_%d" % (a, d), tag="gate")
                 nc.scalar.activation(
                     out=gate[(a, d)][:], in_=acc[(a, d)][:], func=ACT.Sigmoid, bias=bias_bf[:, a : a + 1], scale=1.0
                 )
 
-        def products(i, d):
-            for a in (2 * i, 2 * i + 1):
+        def products(h):
+            for a, d in step_items(h):
                 prod[(a, d)] = prod_pool.tile([P, N], F32, name="prod%d_%d" % (a, d), tag="prod")
                 nc.vector.scalar_tensor_tensor(
-                    out=prod[(a, d)][:], in0=gate[(a, d)][:], scalar=ws_bf[:, d : d + 1], in1=tanh_c[(i, d)][:, a % 2, :],
+                    out=prod[(a, d)][:], in0=gate[(a, d)][:], scalar=ws_bf[:, d : d + 1], in1=tanh_c[(a // 2, d)][:, a % 2, :],
                     op0=ALU.mult, op1=ALU.mult,
                 )
 
-        def sums(i):
-            for a in (2 * i, 2 * i + 1):
-                cols = slice(a * N, (a + 1) * N)
-                nc.vector.tensor_tensor(out=out_sb[:, cols], in0=prod[(a, 0)][:], in1=prod[(a, 1)][:], op=ALU.add)
-                nc.sync.dma_start(out=out0_view[:, a, :], in_=out_sb[:, cols])
+        def store_tile(a):
+            nc.sync.dma_start(out=out0_view[:, a, :], in_=out_sb[:, a * N : (a + 1) * N])
+
+        def add_on_vector(a):
+            nc.vector.tensor_tensor(
+                out=out_sb[:, a * N : (a + 1) * N], in0=prod[(a, 0)][:], in1=prod[(a, 1)][:], op=ALU.add
+            )
+            store_tile(a)
+
+        def add_on_tensor(a):
+            tile_sum[a] = acc_pool.tile([P, N], F32, name="tile_sum%d" % a, tag="acc")
+            for d in range(2):
+                nc.tensor.matmul(
+                    out=tile_sum[a][:], lhsT=ident[:], rhs=prod[(a, d)][:], start=(d == 0), stop=(d == 1)
+                )
+
+        def copy_sum(a):
+            nc.scalar.copy(out=out_sb[:, a * N : (a + 1) * N], in_=tile_sum[a][:])
+            store_tile(a)
 
         def maxima(i):
             if i < PAIRS - 1:
@@ -265,12 +294,12 @@ def tile_mdlstmcellweights_pb_kernel(
         warm(2)
         quantize_wh(0)
         quantize_unit(2)
-        matmuls(0, 0)
-        tanh_pair(0, 0)
+        matmuls(0)
+        tanh_step(0)
         interleave(3)
         interleave(4)
         quantize_unit(3)
-        gates(0, 0)
+        gates(0)
         quantize_unit(4)
 
         late = {}
@@ -283,20 +312,26 @@ def tile_mdlstmcellweights_pb_kernel(
                     nc.tensor.matmul(out=late["sum"][:], lhsT=ident[:], rhs=columns, start=True, stop=True)
 
         for h in range(2 * PAIRS):
-            i, d = h // 2, h % 2
+            i = h // 2
             nxt = h + 1
             if nxt < PAIRS:
                 turn_pair(nxt)
             if nxt < 2 * PAIRS:
-                matmuls(nxt // 2, nxt % 2)
+                matmuls(nxt)
             if h > 0:
-                gates(i, d)
-            products(i, d)
-            if i == PAIRS - 1:
-                keep_clock([prod[(a, d)][:, 0:P] for a in (2 * i, 2 * i + 1)])
-            if d == 1:
-                sums(i)
-            elif i > 0:
+                gates(h)
+            products(h)
+            if h == 2 * PAIRS - 2:
+                keep_clock([out_sb[:, a * N : a * N + P] for a in (TILES - 4, TILES - 3)])
+                add_on_tensor(TILES - 2)
+            elif h == 2 * PAIRS - 1:
+                keep_clock([prod[(TILES - 1, d)][:, 0:P] for d in range(2)])
+                copy_sum(TILES - 2)
+                add_on_vector(TILES - 1)
+            elif h % 2 == 1:
+                add_on_vector(2 * i)
+                add_on_vector(2 * i + 1)
+            if h % 2 == 0 and i > 0:
                 maxima(i - 1)
             if nxt < PAIRS:
                 copy_wh(2 * nxt)
@@ -304,7 +339,7 @@ def tile_mdlstmcellweights_pb_kernel(
                 copy_wi("vector" if nxt < PAIRS - 1 else "scalar", nxt)
                 quantize_pair(nxt)
             if nxt < 2 * PAIRS:
-                tanh_pair(nxt // 2, nxt % 2)
+                tanh_step(nxt)
         keep_clock([out_sb[:, a * N : a * N + P] for a in (TILES - 2, TILES - 1)])
         maxima(PAIRS - 1)
 

from contextlib import ExitStack

import concourse.mybir as mybir
from concourse.masks import make_identity

IN_C, OUT_C, N = 512, 1024, 512
FLOPS = 2 * OUT_C * IN_C * N + 2 * 2 * OUT_C * OUT_C * N

F32 = mybir.dt.float32
BF16 = mybir.dt.bfloat16
U32 = mybir.dt.uint32
U8 = mybir.dt.uint8
FP8X4 = mybir.dt.float8_e4m3fn_x4
FP8 = mybir.dt.float8_e4m3fn
ACT = mybir.ActivationFunctionType
ALU = mybir.AluOpType
AX = mybir.AxisListType

P = 128
PACK = 4
K_PASS = P * PACK
TILES = OUT_C // P
PAIRS = TILES // 2
UNITS = 5
N_VECTOR = (384,384,384,384,448)
CASTS = (("vector", 0, 1024), ("scalar", 2752, 3424), ("vector", 1024, 2048), ("scalar", 3424, 4096), ("vector", 2048, 2752))


def tile_mdlstmcellweights_pb_kernel(
    tc, x, h_prev_dim0, h_prev_dim1, ct0, ct1, w_io, w_ho, b_o, weighted_sum, out_0, out_1
):
    nc = tc.nc
    with ExitStack() as ctx:
        keep = ctx.enter_context(tc.tile_pool(name="keep", bufs=1))
        gate_pool = ctx.enter_context(tc.tile_pool(name="gate_pool", bufs=6))
        prod_pool = ctx.enter_context(tc.tile_pool(name="prod_pool", bufs=6))
        turn_pool = ctx.enter_context(tc.psum_pool(name="turn_pool", bufs=3))
        acc_pool = ctx.enter_context(tc.psum_pool(name="acc_pool", bufs=5))
        ctx.enter_context(tc.manual_schedule())

        bias_bf = keep.tile([P, TILES], BF16, name="bias_bf")
        ws_bf = keep.tile([P, 2], BF16, name="ws_bf")
        nc.scalar.dma_start(out=bias_bf[:], in_=b_o.rearrange("(p a) o -> p (a o)", a=TILES))
        nc.scalar.dma_start(out=ws_bf[:], in_=weighted_sum.partition_broadcast(P))

        zeros = keep.tile([P, 1], F32, name="zeros")
        nc.vector.memset(zeros[:], 0.0)
        first_act = keep.tile([P, 1], F32, name="first_act")
        nc.scalar.activation(out=first_act[:], in_=zeros[:], func=ACT.Sigmoid)
        ident = keep.tile([P, P], F32, name="ident")
        make_identity(nc, ident[:])

        unit_src = ((x, 0), (h_prev_dim0, 0), (h_prev_dim0, 1), (h_prev_dim1, 0), (h_prev_dim1, 1))
        raw = [keep.tile([P, PACK, N], BF16, name="raw%d" % u) for u in range(UNITS)]
        wh_raw = [keep.tile([P, 2, OUT_C], BF16, name="wh_raw%d" % i) for i in range(PAIRS)]
        wi_raw = [keep.tile([P, 2, IN_C], BF16, name="wi_raw%d" % i) for i in range(PAIRS)]
        ct_raw = [[keep.tile([P, 2, N], BF16, name="ct%d_raw%d" % (d, i)) for i in range(PAIRS)] for d in range(2)]
        wh_view = w_ho.rearrange("(p a) k -> p a k", a=TILES)
        wi_view = w_io.rearrange("(p a) k -> p a k", a=TILES)
        ct_view = (ct0.rearrange("(p a) n -> p a n", a=TILES), ct1.rearrange("(p a) n -> p a n", a=TILES))

        def load_unit(u):
            src, g = unit_src[u]
            rows = src[K_PASS * g : K_PASS * (g + 1), :]
            nc.sync.dma_start(out=raw[u][:], in_=rows.rearrange("(p j) n -> p j n", j=PACK))

        def load_wh(i):
            nc.sync.dma_start(out=wh_raw[i][:], in_=wh_view[:, 2 * i : 2 * i + 2, :])

        def load_wh_tiles(i):
            for j in range(2):
                nc.sync.dma_start(out=wh_raw[i][:, j, :], in_=wh_view[:, 2 * i + j, :])

        def load_wi(i):
            nc.sync.dma_start(out=wi_raw[i][:], in_=wi_view[:, 2 * i : 2 * i + 2, :])

        def load_ct(d, i):
            nc.sync.dma_start(out=ct_raw[d][i][:], in_=ct_view[d][:, 2 * i : 2 * i + 2, :])

        load_wi(0)
        load_unit(0)
        load_unit(1)
        load_wh_tiles(0)
        load_unit(2)
        load_ct(0, 0)
        load_unit(3)
        load_unit(4)
        load_wh_tiles(1)
        load_wi(1)
        load_ct(1, 0)
        load_wh(2)
        load_ct(0, 1)
        load_wi(2)
        load_wh(3)
        load_wi(3)
        load_ct(1, 1)
        for i in range(2, PAIRS):
            load_ct(0, i)
            load_ct(1, i)

        grouped = [keep.tile([P, N, PACK], BF16, name="grouped%d" % u, align_bytes=64) for u in range(UNITS)]
        unit_codes = [keep.tile([P, N], U32, name="unit_codes%d" % u, align_bytes=64) for u in range(UNITS)]
        unit_scales = [keep.tile([P, N], U8, name="unit_scales%d" % u, align_bytes=64) for u in range(UNITS)]

        def interleave(u):
            nc.vector.tensor_copy(
                out=grouped[u][:, 0:N_VECTOR[u], :], in_=raw[u][:, :, 0:N_VECTOR[u]].rearrange("p j n -> p n j")
            )
            nc.scalar.copy(out=grouped[u][:, N_VECTOR[u]:N, :], in_=raw[u][:, :, N_VECTOR[u]:N].rearrange("p j n -> p n j"))

        def quantize_unit(u):
            nc.vector.quantize_mx(
                out=unit_codes[u][:].bitcast(FP8X4),
                scales=unit_scales[u][:],
                in_=grouped[u][:].rearrange("p n j -> p (n j)"),
            )

        def warm_ident(n):
            idle_sum = acc_pool.tile([P, P], F32, name="early_sum", tag="acc")
            for j in range(n):
                nc.tensor.matmul(out=idle_sum[:], lhsT=ident[:], rhs=ident[:], start=True, stop=True)

        def warm(u):
            idle_sum = acc_pool.tile([P, N], F32, name="idle_sum%d" % u, tag="acc")
            for j in range(2):
                nc.tensor.matmul(out=idle_sum[:], lhsT=raw[u][:, j, 0:P], rhs=raw[u][:, 2 + j, :], start=True, stop=True)

        wh_grouped = [keep.tile([P, 4 * K_PASS], BF16, name="wh_grouped%d" % i, align_bytes=64) for i in range(PAIRS)]
        wi_grouped = [keep.tile([P, 2 * K_PASS], BF16, name="wi_grouped%d" % i, align_bytes=64) for i in range(PAIRS)]
        wh_codes = [keep.tile([P, 4 * P], U32, name="wh_codes%d" % i, align_bytes=64) for i in range(PAIRS)]
        wh_scales = [keep.tile([P, 4 * P], U8, name="wh_scales%d" % i, align_bytes=64) for i in range(PAIRS)]
        wi_codes = [keep.tile([P, 2 * P], U32, name="wi_codes%d" % i, align_bytes=64) for i in range(PAIRS)]
        wi_scales = [keep.tile([P, 2 * P], U8, name="wi_scales%d" % i, align_bytes=64) for i in range(PAIRS)]
        turned = {}

        def turn(name, sources):
            bank = turn_pool.tile([P, 2, 2, P], F32, name="turned_%s" % name, tag="turned")
            for s, (rows, g) in enumerate(sources):
                words = rows.bitcast(F32)
                for u in range(2):
                    nc.tensor.transpose(bank[:, s, u, :], words[:, 256 * g + u : 256 * (g + 1) : 2], ident[:])
            turned[name] = bank

        def turn_wh(a):
            rows = wh_raw[a // 2][:, a % 2, :]
            turn("h%d" % a, ((rows, 0), (rows, 1)))

        def turn_wi(i):
            turn("i%d" % i, ((wi_raw[i][:, 0, :], 0), (wi_raw[i][:, 1, :], 0)))

        def turn_pair(i):
            turn_wh(2 * i)
            turn_wh(2 * i + 1)
            turn_wi(i)

        def copy_out(engine, name, dst):
            out = dst.bitcast(F32).rearrange("p (s r u) -> p s r u", s=2, u=2)
            in_ = turned[name][:].rearrange("p s u r -> p s r u")
            if engine == "vector":
                nc.vector.tensor_copy(out=out, in_=in_)
            else:
                nc.scalar.copy(out=out, in_=in_)

        def copy_wh(a):
            copy_out("scalar", "h%d" % a, wh_grouped[a // 2][:, 2 * K_PASS * (a % 2) : 2 * K_PASS * (a % 2 + 1)])

        def copy_wi(engine, i):
            copy_out(engine, "i%d" % i, wi_grouped[i][:])

        def quantize_wh(i):
            nc.vector.quantize_mx(out=wh_codes[i][:].bitcast(FP8X4), scales=wh_scales[i][:], in_=wh_grouped[i][:])

        def quantize_wi(i):
            nc.vector.quantize_mx(out=wi_codes[i][:].bitcast(FP8X4), scales=wi_scales[i][:], in_=wi_grouped[i][:])

        def quantize_pair(i):
            quantize_wh(i)
            quantize_wi(i)

        acc = {}
        gate = {}
        prod = {}
        tile_sum = {}
        out_sb = keep.tile([P, TILES * N + 8], F32, name="out_sb")
        out0_view = out_0.rearrange("(p a) n -> p a n", a=TILES)
        out1_view = out_1.rearrange("(p a) n -> p (a n)", a=TILES)
        part_max = keep.tile([P, 1], F32, name="part_max")

        def step_items(h):
            i, j = h // 2, h % 2
            if i < PAIRS - 1:
                return [(2 * i, j), (2 * i + 1, j)]
            return [(2 * i + j, 0), (2 * i + j, 1)]

        tanh_c = {
            (i, d): keep.tile([P, 2, N], F32, name="tanh_c%d_%d" % (i, d)) for i in range(PAIRS) for d in range(2)
        }

        def tanh_step(h):
            i, j = h // 2, h % 2
            if i < PAIRS - 1:
                nc.scalar.activation(out=tanh_c[(i, j)][:], in_=ct_raw[j][i][:], func=ACT.Tanh)
            else:
                for d in range(2):
                    nc.scalar.activation(out=tanh_c[(i, d)][:, j, :], in_=ct_raw[d][i][:, j, :], func=ACT.Tanh)

        def matmuls(h):
            for a, d in step_items(h):
                i = a // 2
                acc[(a, d)] = acc_pool.tile([P, N], F32, name="acc%d_%d" % (a, d), tag="acc")
                half = a % 2
                passes = (
                    (wi_codes[i], wi_scales[i], half, 0),
                    (wh_codes[i], wh_scales[i], 2 * half, 1 + 2 * d),
                    (wh_codes[i], wh_scales[i], 2 * half + 1, 2 + 2 * d),
                )
                for s, (codes, scales, c, u) in enumerate(passes):
                    nc.tensor.matmul_mx(
                        out=acc[(a, d)][:],
                        lhsT=codes[:, c * P : (c + 1) * P].bitcast(FP8X4),
                        lhsT_scale=scales[:, c * P : (c + 1) * P],
                        rhs=unit_codes[u][:].bitcast(FP8X4),
                        rhs_scale=unit_scales[u][:],
                        start=(s == 0),
                        stop=(s == 2),
                    )

        def gates(h):
            for a, d in step_items(h):
                gate[(a, d)] = gate_pool.tile([P, N], F32, name="gate%d_%d" % (a, d), tag="gate")
                nc.scalar.activation(
                    out=gate[(a, d)][:], in_=acc[(a, d)][:], func=ACT.Sigmoid, bias=bias_bf[:, a : a + 1], scale=1.0
                )

        def products(h):
            for a, d in step_items(h):
                prod[(a, d)] = prod_pool.tile([P, N], F32, name="prod%d_%d" % (a, d), tag="prod")
                nc.vector.scalar_tensor_tensor(
                    out=prod[(a, d)][:], in0=gate[(a, d)][:], scalar=ws_bf[:, d : d + 1], in1=tanh_c[(a // 2, d)][:, a % 2, :],
                    op0=ALU.mult, op1=ALU.mult,
                )

        def store_tile(a):
            nc.sync.dma_start(out=out0_view[:, a, :], in_=out_sb[:, a * N : (a + 1) * N])

        def add_on_vector(a):
            nc.vector.tensor_tensor(
                out=out_sb[:, a * N : (a + 1) * N], in0=prod[(a, 0)][:], in1=prod[(a, 1)][:], op=ALU.add
            )
            store_tile(a)

        def add_on_tensor(a):
            tile_sum[a] = acc_pool.tile([P, N], F32, name="tile_sum%d" % a, tag="acc")
            for d in range(2):
                nc.tensor.matmul(
                    out=tile_sum[a][:], lhsT=ident[:], rhs=prod[(a, d)][:], start=(d == 0), stop=(d == 1)
                )

        def copy_sum(a):
            nc.scalar.copy(out=out_sb[:, a * N : (a + 1) * N], in_=tile_sum[a][:])
            store_tile(a)

        def maxima(i):
            if i < PAIRS - 1:
                nc.vector.tensor_reduce(
                    out=out_sb[:, TILES * N + i : TILES * N + i + 1], in_=out_sb[:, 2 * i * N : (2 * i + 2) * N],
                    axis=AX.X, op=ALU.max, apply_absolute_value=True,
                )
            else:
                nc.vector.tensor_reduce(
                    out=out_sb[:, TILES * N + i : TILES * N + i + 1], in_=out_sb[:, 2 * i * N : (2 * i + 1) * N],
                    axis=AX.X, op=ALU.max, apply_absolute_value=True,
                )
                nc.vector.tensor_reduce(
                    out=part_max[:], in_=out_sb[:, (2 * i + 1) * N : TILES * N + PAIRS],
                    axis=AX.X, op=ALU.max, apply_absolute_value=True,
                )

        warm_ident(3)
        turn_wi(0)
        copy_wi("scalar", 0)
        interleave(0)
        warm(0)
        quantize_wi(0)
        interleave(1)
        warm(1)
        quantize_unit(0)
        turn_wh(0)
        turn_wh(1)
        quantize_unit(1)
        copy_wh(0)
        copy_wh(1)
        interleave(2)
        warm(2)
        quantize_wh(0)
        quantize_unit(2)
        matmuls(0)
        tanh_step(0)
        interleave(3)
        interleave(4)
        quantize_unit(3)
        gates(0)
        quantize_unit(4)

        late = {}

        def keep_clock(fresh):
            if not late:
                late["sum"] = turn_pool.tile([P, P], F32, name="late_sum", tag="turned")
            for columns in fresh:
                for j in range(2):
                    nc.tensor.matmul(out=late["sum"][:], lhsT=ident[:], rhs=columns, start=True, stop=True)

        for h in range(2 * PAIRS):
            i = h // 2
            nxt = h + 1
            if nxt < PAIRS:
                turn_pair(nxt)
            if nxt < 2 * PAIRS:
                matmuls(nxt)
            if h > 0:
                gates(h)
            products(h)
            if h == 2 * PAIRS - 2:
                keep_clock([out_sb[:, a * N : a * N + P] for a in (TILES - 4, TILES - 3)])
                add_on_tensor(TILES - 2)
            elif h == 2 * PAIRS - 1:
                keep_clock([prod[(TILES - 1, d)][:, 0:P] for d in range(2)])
                copy_sum(TILES - 2)
                add_on_vector(TILES - 1)
            elif h % 2 == 1:
                add_on_vector(2 * i)
                add_on_vector(2 * i + 1)
            if h % 2 == 0 and i > 0:
                maxima(i - 1)
            if nxt < PAIRS:
                copy_wh(2 * nxt)
                copy_wh(2 * nxt + 1)
                copy_wi("vector" if nxt < PAIRS - 1 else "scalar", nxt)
                quantize_pair(nxt)
            if nxt < 2 * PAIRS:
                tanh_step(nxt)
        keep_clock([out_sb[:, a * N : a * N + P] for a in (TILES - 2, TILES - 1)])
        maxima(PAIRS - 1)

        spread = turn_pool.tile([P, P], F32, name="spread", tag="turned")
        nc.tensor.transpose(spread[:], part_max[:, 0:1].to_broadcast([P, P]), ident[:])
        scaled = keep.tile([P, P], F32, name="scaled")
        scale = keep.tile([P, 1], F32, name="scale")
        nc.vector.tensor_scalar(
            out=scaled[:], in0=spread[:], scalar1=1.0 / 448.0, scalar2=None, op0=ALU.mult, op1=ALU.max, accum_out=scale[:]
        )
        factor = keep.tile([P, 1], F32, name="factor")
        nc.vector.reciprocal(out=factor[:], in_=scale[:])

        for engine, c0, c1 in CASTS:
            codes8 = keep.tile([P, c1 - c0], FP8, name="codes8_%d" % c0)
            if engine == "vector":
                nc.vector.tensor_scalar(
                    out=codes8[:], in0=out_sb[:, c0:c1], scalar1=factor[:, 0:1], scalar2=None, op0=ALU.mult,
                    saturate=False,
                )
            else:
                nc.scalar.activation(
                    out=codes8[:], in_=out_sb[:, c0:c1], func=ACT.Identity, scale=factor[:, 0:1], bias=zeros[:, 0:1],
                    saturate=False,
                )
            nc.sync.dma_start(out=out1_view[:, c0:c1], in_=codes8[:].bitcast(U8))
